import numpy as np
import ml_dtypes


def mxq(x, axis, fmt="e4m3"):
    dtype, down = {"e4m3": (ml_dtypes.float8_e4m3fn, 7), "e5m2": (ml_dtypes.float8_e5m2, 14)}[fmt]
    v = np.moveaxis(np.asarray(x, np.float32).astype(ml_dtypes.bfloat16).astype(np.float64), axis, -1)
    blocks = v.reshape(v.shape[:-1] + (-1, 32))
    amax = np.abs(blocks).max(-1, keepdims=True)
    byte = np.maximum(np.where(amax > 0, np.frexp(amax)[1] - 1 + 127, 0) - down, 1)
    scale = np.exp2(byte - 127.0)
    codes = (blocks / scale).astype(np.float32).astype(dtype).astype(np.float64)
    return np.moveaxis((codes * scale).reshape(v.shape), -1, axis)


WIDE = False


def mx_kscale(k):
    if not WIDE:
        return np.ones(k)
    levels = np.array([10, -10, 5, -5, 0])
    a = np.random.permutation(np.resize(levels, k // 512 * 4)).reshape(k // 512, 4)
    idx = np.arange(k)
    return np.exp2(a[idx // 512, idx % 128 // 32])


BF16 = ml_dtypes.bfloat16


def bf(x):
    return np.asarray(x, np.float32).astype(BF16)


def f64(x):
    return np.asarray(x).astype(np.float64)


B, H, W, C = 128, 5, 5, 1024
PIXEL = 2
STEP = 1
EPS = 1e-6
PAD = (PIXEL - H % PIXEL) % PIXEL
HP = H + PAD
R = HP // PIXEL
K1 = PIXEL * C
F = C // 2


def layer_norm(v, g, b):
    m = v.mean(-1, keepdims=True)
    var = np.square(v - m).mean(-1, keepdims=True)
    return (v - m) / np.sqrt(var + EPS) * g + b


def setup_inputs():
    s = mx_kscale(C)
    t = mx_kscale(F)
    return {
        "x": bf(np.random.standard_normal((B, H, W, C)) * s),
        "wh1": bf(np.random.standard_normal((K1, F)) / np.sqrt(K1) / np.tile(s, PIXEL)[:, None]),
        "gh": bf((1.0 + 0.1 * np.random.standard_normal(F)) * t),
        "bh": bf(0.2 * np.random.standard_normal(F) * t),
        "wh2": bf(np.random.standard_normal((F, K1)) / np.sqrt(F) / t[:, None]),
        "bh2": bf(0.3 * np.random.standard_normal(K1)),
    }


def reference(x, wh1, gh, bh, wh2, bh2):
    r = np.roll(f64(x), STEP, axis=1)
    r = np.concatenate([r[:, -PAD:], r], axis=1)
    z = r.reshape(B, PIXEL, R, W, C).transpose(0, 2, 3, 1, 4).reshape(B, R, W, K1)
    u = mxq(z, 3, "e4m3") @ mxq(f64(wh1), 0, "e4m3")
    hid = np.maximum(layer_norm(u, f64(gh), f64(bh)), 0.0)
    y = (mxq(hid, 3, "e4m3") @ mxq(f64(wh2), 0, "e4m3")) + f64(bh2)
    y = y.reshape(B, R, W, PIXEL, C).transpose(0, 3, 1, 2, 4).reshape(B, HP, W, C)[:, PAD:]
    return np.roll(y, -STEP, axis=1)

@@ -1,0 +1,283 @@
+from contextlib import ExitStack
+
+import concourse.mybir as mybir
+from concourse.masks import make_identity
+
+F32 = mybir.dt.float32
+BF16 = mybir.dt.bfloat16
+U32 = mybir.dt.uint32
+U8 = mybir.dt.uint8
+FP8X4 = mybir.dt.float8_e4m3fn_x4
+ACT = mybir.ActivationFunctionType
+ALU = mybir.AluOpType
+
+P = 128
+PACK = 4
+K_PASS = P * PACK
+N_TILE = 512
+
+B, H, W, C = 128, 5, 5, 1024
+PIXEL = 2
+R = 3
+K1 = PIXEL * C
+F = C // 2
+EPS = 1e-6
+ROW_PASSES = C // K_PASS
+W1_PASSES = K1 // K_PASS
+W2_BLOCKS = K1 // N_TILE
+ROW_BLOCKS = C // N_TILE
+
+FLOPS = 2 * B * R * W * (K1 * F + F * K1)
+
+
+def image_row(j, pixel):
+    return (j + R * pixel + 3) % H
+
+
+def tile_hiremodule_pa_kernel(tc, x, wh1, gh, bh, wh2, bh2, out):
+    nc = tc.nc
+    regions = [(w, j) for w in range(W) for j in range(R)]
+    with ExitStack() as ctx:
+        ctx.enter_context(tc.manual_schedule())
+        consts = ctx.enter_context(tc.tile_pool(name="consts", bufs=1))
+        x_pool = ctx.enter_context(tc.tile_pool(name="x_pool", bufs=H * W))
+        stage = ctx.enter_context(tc.tile_pool(name="stage", bufs=3))
+        work = ctx.enter_context(tc.tile_pool(name="work", bufs=3))
+        x_code_pool = ctx.enter_context(tc.tile_pool(name="x_code_pool", bufs=2 * H))
+        out_pool = ctx.enter_context(tc.tile_pool(name="out_pool", bufs=6))
+        psum_x = ctx.enter_context(tc.psum_pool(name="psum_x", bufs=2))
+        psum_u = ctx.enter_context(tc.psum_pool(name="psum_u", bufs=2))
+        psum_h = ctx.enter_context(tc.psum_pool(name="psum_h", bufs=1))
+        psum_y = ctx.enter_context(tc.psum_pool(name="psum_y", bufs=3))
+
+        def new_rows(j):
+            rows = [image_row(j, pixel) for pixel in range(PIXEL)]
+            return [h for h in rows if j == 0 or h != image_row(0, 0)]
+
+        x_rows = {}
+
+        def load_x(w):
+            for j in range(R):
+                for h in new_rows(j):
+                    x_row = x_pool.tile([P, C], BF16)
+                    nc.sync.dma_start(out=x_row[:], in_=x[:, h, w, :])
+                    x_rows[(w, h)] = x_row
+
+        gain_rows = consts.tile([P, P], BF16)
+        nc.vector.memset(gain_rows[:], 0.0)
+        nc.sync.dma_start(out=gain_rows[0:PACK, :], in_=gh.rearrange("(t p) -> t p", p=P))
+        nc.sync.dma_start(out=gain_rows[PACK : 2 * PACK, :], in_=bh.rearrange("(t p) -> t p", p=P))
+        w1_raw = consts.tile([P, W1_PASSES, PACK, F], BF16)
+        for c in range(W1_PASSES):
+            nc.sync.dma_start(
+                out=w1_raw[:, c].rearrange("p (u e) f -> p u (e f)", e=2),
+                in_=wh1[c * K_PASS : (c + 1) * K_PASS, :].rearrange(
+                    "(u p e) f -> p u (e f)", u=2, p=P, e=2
+                ),
+            )
+        load_x(0)
+        w2_order = [(k + W2_BLOCKS // 2) % W2_BLOCKS for k in range(W2_BLOCKS)]
+        w2_raw = consts.tile([P, W2_BLOCKS, PACK, N_TILE], BF16)
+        for n in w2_order:
+            nc.sync.dma_start(
+                out=w2_raw[:, n],
+                in_=wh2[:, n * N_TILE : (n + 1) * N_TILE].rearrange("(t p) c -> p t c", p=P),
+            )
+        bias2 = consts.tile([P, K1], BF16)
+        nc.sync.dma_start(out=bias2[:], in_=bh2.partition_broadcast(P))
+        for w in range(1, W):
+            load_x(w)
+
+        ident = consts.tile([P, P], F32)
+        make_identity(nc, ident[:])
+        eps = consts.tile([P, 1], F32)
+        nc.vector.memset(eps[:], EPS)
+
+        gain_rows_f32 = consts.tile([P, P], F32)
+        nc.vector.tensor_copy(out=gain_rows_f32[:], in_=gain_rows[:])
+        gain_t = psum_h.tile([P, PACK, P], F32, tag="hid_t")
+        nc.tensor.transpose(gain_t[:, 0, :], gain_rows_f32[:], ident[:])
+        gain_cols = consts.tile([P, 2 * PACK], F32)
+        nc.vector.tensor_copy(out=gain_cols[:], in_=gain_t[:, 0, 0 : 2 * PACK])
+
+        def regroup_weight_block(raw):
+            grouped = stage.tile([P, N_TILE, PACK], BF16, align_bytes=64, tag="w_grouped")
+            half = N_TILE // 2
+            nc.vector.tensor_copy(
+                out=grouped[:, :half, :].rearrange("p (c i) t -> p c t i", i=4),
+                in_=raw[:, :, :half].rearrange("p t (c i) -> p c t i", i=4),
+            )
+            nc.scalar.copy(
+                out=grouped[:, half:, :].rearrange("p (c i) t -> p c t i", i=4),
+                in_=raw[:, :, half:].rearrange("p t (c i) -> p c t i", i=4),
+            )
+            return grouped
+
+        def quantise_weight_block(grouped, codes, scales):
+            nc.vector.quantize_mx(
+                out=codes.bitcast(FP8X4),
+                scales=scales,
+                in_=grouped[:].rearrange("p c t -> p (c t)"),
+            )
+
+        w1_codes = consts.tile([P, W1_PASSES, F], U32, align_bytes=64)
+        w1_scales = consts.tile([P, W1_PASSES, F], U8, align_bytes=64)
+        w1_grouped = {}
+        for c in range(W1_PASSES + 1):
+            if c < W1_PASSES:
+                w1_grouped[c] = regroup_weight_block(w1_raw[:, c])
+            if c > 0:
+                quantise_weight_block(w1_grouped[c - 1], w1_codes[:, c - 1, :], w1_scales[:, c - 1, :])
+        w2_codes = consts.tile([P, W2_BLOCKS, N_TILE], U32, align_bytes=64)
+        w2_scales = consts.tile([P, W2_BLOCKS, N_TILE], U8, align_bytes=64)
+
+        x_t, x_grouped, x_codes, x_scales = {}, {}, {}, {}
+        u_bank, mean_var, norms, hid_ts, hid_planes, hid_codes, hid_scales = {}, {}, {}, {}, {}, {}, {}
+
+        def transpose_x(n):
+            w, j = regions[n]
+            for h in new_rows(j):
+                x_words = x_rows[(w, h)][:].bitcast(F32)
+                bank = psum_x.tile([P, 2 * ROW_PASSES, P], F32)
+                for q in range(2 * ROW_PASSES):
+                    nc.tensor.transpose(bank[:, q, :], x_words[:, q * P : (q + 1) * P], ident[:])
+                x_t[(w, h)] = bank
+
+        def copy_x(n):
+            w, j = regions[n]
+            for h in new_rows(j):
+                grouped = stage.tile([P, ROW_PASSES, P, 2], F32, align_bytes=64, tag="x_grouped")
+                nc.scalar.copy(
+                    out=grouped[:], in_=x_t[(w, h)][:].rearrange("p (g u) b -> p g b u", u=2)
+                )
+                x_grouped[(w, h)] = grouped
+
+        def quantise_x(n):
+            w, j = regions[n]
+            for h in new_rows(j):
+                codes = x_code_pool.tile([P, ROW_PASSES, P], U32, align_bytes=64, tag="x_codes")
+                scales = x_code_pool.tile([P, ROW_PASSES, P], U8, align_bytes=64, tag="x_scales")
+                nc.vector.quantize_mx(
+                    out=codes[:].rearrange("p g b -> p (g b)").bitcast(FP8X4),
+                    scales=scales[:].rearrange("p g b -> p (g b)"),
+                    in_=x_grouped[(w, h)][:].rearrange("p g b u -> p (g b u)").bitcast(BF16),
+                )
+                x_codes[(w, h)], x_scales[(w, h)] = codes, scales
+
+        def first_matmul(n):
+            w, j = regions[n]
+            u = psum_u.tile([P, F], F32)
+            for c in range(W1_PASSES):
+                h = image_row(j, c // ROW_PASSES)
+                g = c % ROW_PASSES
+                nc.tensor.matmul_mx(
+                    out=u[:],
+                    lhsT=x_codes[(w, h)][:, g, :].bitcast(FP8X4),
+                    lhsT_scale=x_scales[(w, h)][:, g, :],
+                    rhs=w1_codes[:, c, :].bitcast(FP8X4),
+                    rhs_scale=w1_scales[:, c, :],
+                    start=(c == 0),
+                    stop=(c == W1_PASSES - 1),
+                )
+            u_bank[n] = u
+
+        def statistics(n):
+            stats = work.tile([P, 6], F32)
+            nc.vector.bn_stats(out=stats[:], in_=u_bank[n][:])
+            mv = work.tile([P, 2], F32)
+            nc.vector.bn_aggr(out=mv[:], in_=stats[:])
+            mean_var[n] = mv
+
+        def normalise(n):
+            mv = mean_var[n]
+            rstd = work.tile([P, 1], F32)
+            nc.scalar.activation(
+                out=rstd[:], in_=mv[:, 1:2], func=ACT.Abs_reciprocal_sqrt, bias=eps[:]
+            )
+            shift = work.tile([P, 1], F32)
+            nc.scalar.activation(out=shift[:], in_=mv[:, 0:1], func=ACT.Copy, scale=rstd[:])
+            nc.scalar.mul(out=shift[:], in_=shift[:], mul=-1.0)
+            norm = work.tile([P, F], F32)
+            nc.scalar.activation(
+                out=norm[:], in_=u_bank[n][:], func=ACT.Identity, scale=rstd[:], bias=shift[:]
+            )
+            norms[n] = norm
+
+        def transpose_hidden(n):
+            hid_t = psum_h.tile([P, PACK, P], F32, tag="hid_t")
+            for t in range(PACK):
+                nc.tensor.transpose(hid_t[:, t, :], norms[n][:, t * P : (t + 1) * P], ident[:])
+            hid_ts[n] = hid_t
+
+        def activate_hidden(n):
+            planes = work.tile([P, PACK, P], BF16)
+            for t in range(PACK):
+                nc.scalar.activation(
+                    out=planes[:, t, :], in_=hid_ts[n][:, t, :], func=ACT.Relu,
+                    scale=gain_cols[:, t : t + 1], bias=gain_cols[:, PACK + t : PACK + t + 1],
+                )
+            hid_planes[n] = planes
+
+        def quantise_hidden(n):
+            grouped = work.tile([P, P, PACK], BF16, align_bytes=64, tag="hid_grouped")
+            nc.vector.tensor_copy(
+                out=grouped[:].rearrange("p (c i) t -> p c t i", i=4),
+                in_=hid_planes[n][:].rearrange("p t (c i) -> p c t i", i=4),
+            )
+            codes = work.tile([P, P], U32, align_bytes=64, tag="hid_codes")
+            scales = work.tile([P, P], U8, align_bytes=64, tag="hid_scales")
+            nc.vector.quantize_mx(
+                out=codes[:].bitcast(FP8X4),
+                scales=scales[:],
+                in_=grouped[:].rearrange("p b t -> p (b t)"),
+            )
+            hid_codes[n], hid_scales[n] = codes, scales
+
+        def second_matmul(n):
+            w, j = regions[n]
+            for pixel in range(PIXEL):
+                if j == 0 and pixel == 0:
+                    continue
+                result = out_pool.tile([P, C], F32)
+                for half in range(ROW_BLOCKS):
+                    block = pixel * ROW_BLOCKS + half
+                    y = psum_y.tile([P, N_TILE], F32)
+                    nc.tensor.matmul_mx(
+                        out=y[:],
+                        lhsT=hid_codes[n][:].bitcast(FP8X4),
+                        lhsT_scale=hid_scales[n][:],
+                        rhs=w2_codes[:, block, :].bitcast(FP8X4),
+                        rhs_scale=w2_scales[:, block, :],
+                        start=True,
+                        stop=True,
+                    )
+                    nc.vector.tensor_tensor(
+                        out=result[:, half * N_TILE : (half + 1) * N_TILE],
+                        in0=y[:],
+                        in1=bias2[:, block * N_TILE : (block + 1) * N_TILE],
+                        op=ALU.add,
+                    )
+                nc.sync.dma_start(out=out[:, image_row(j, pixel), w, :], in_=result[:])
+
+        def run(stage_of_region, n):
+            if 0 <= n < len(regions):
+                stage_of_region(n)
+
+        w2_grouped = {}
+        for step in range(len(regions) + 5):
+            run(transpose_x, step)
+            run(quantise_hidden, step - 4)
+            run(copy_x, step)
+            run(quantise_x, step)
+            run(first_matmul, step - 1)
+            run(statistics, step - 1)
+            if 1 <= step <= W2_BLOCKS:
+                n = w2_order[step - 1]
+                quantise_weight_block(w2_grouped[n], w2_codes[:, n, :], w2_scales[:, n, :])
+            run(normalise, step - 2)
+            run(transpose_hidden, step - 3)
+            if step < W2_BLOCKS:
+                n = w2_order[step]
+                w2_grouped[n] = regroup_weight_block(w2_raw[:, n])
+            run(activate_hidden, step - 3)
+            run(second_matmul, step - 5)

@@ -78,14 +78,20 @@ def tile_hiremodule_pa_kernel(tc, x, wh1, gh, bh, wh2, bh2, out):
         load_x(0)
         w2_order = [(k + W2_BLOCKS // 2) % W2_BLOCKS for k in range(W2_BLOCKS)]
         w2_raw = consts.tile([P, W2_BLOCKS, PACK, N_TILE], BF16)
-        for n in w2_order:
-            nc.sync.dma_start(
-                out=w2_raw[:, n],
-                in_=wh2[:, n * N_TILE : (n + 1) * N_TILE].rearrange("(t p) c -> p t c", p=P),
-            )
+
+        def load_w2(blocks):
+            for n in blocks:
+                nc.sync.dma_start(
+                    out=w2_raw[:, n],
+                    in_=wh2[:, n * N_TILE : (n + 1) * N_TILE].rearrange("(t p) c -> p t c", p=P),
+                )
+
+        load_w2(w2_order[: W2_BLOCKS // 2])
+        load_x(1)
+        load_w2(w2_order[W2_BLOCKS // 2 :])
         bias2 = consts.tile([P, K1], BF16)
         nc.sync.dma_start(out=bias2[:], in_=bh2.partition_broadcast(P))
-        for w in range(1, W):
+        for w in range(2, W):
             load_x(w)
 
         ident = consts.tile([P, P], F32)

@@ -138,7 +138,8 @@ def tile_hiremodule_pa_kernel(tc, x, wh1, gh, bh, wh2, bh2, out):
         w2_scales = consts.tile([P, W2_BLOCKS, N_TILE], U8, align_bytes=64)
 
         x_t, x_grouped, x_codes, x_scales = {}, {}, {}, {}
-        u_bank, mean_var, norms, hid_ts, hid_planes, hid_codes, hid_scales = {}, {}, {}, {}, {}, {}, {}
+        u_bank, halves, mean_var, norms = {}, {}, {}, {}
+        hid_ts, hid_planes, hid_grouped, hid_codes, hid_scales = {}, {}, {}, {}, {}
 
         def transpose_x(n):
             w, j = regions[n]
@@ -190,8 +191,11 @@ def tile_hiremodule_pa_kernel(tc, x, wh1, gh, bh, wh2, bh2, out):
         def statistics(n):
             stats = work.tile([P, 6], F32)
             nc.vector.bn_stats(out=stats[:], in_=u_bank[n][:])
+            halves[n] = stats
+
+        def aggregate(n):
             mv = work.tile([P, 2], F32)
-            nc.vector.bn_aggr(out=mv[:], in_=stats[:])
+            nc.vector.bn_aggr(out=mv[:], in_=halves[n][:])
             mean_var[n] = mv
 
         def normalise(n):
@@ -224,18 +228,21 @@ def tile_hiremodule_pa_kernel(tc, x, wh1, gh, bh, wh2, bh2, out):
                 )
             hid_planes[n] = planes
 
-        def quantise_hidden(n):
+        def regroup_hidden(n):
             grouped = work.tile([P, P, PACK], BF16, align_bytes=64, tag="hid_grouped")
             nc.vector.tensor_copy(
                 out=grouped[:].rearrange("p (c i) t -> p c t i", i=4),
                 in_=hid_planes[n][:].rearrange("p t (c i) -> p c t i", i=4),
             )
+            hid_grouped[n] = grouped
+
+        def quantise_hidden(n):
             codes = work.tile([P, P], U32, align_bytes=64, tag="hid_codes")
             scales = work.tile([P, P], U8, align_bytes=64, tag="hid_scales")
             nc.vector.quantize_mx(
                 out=codes[:].bitcast(FP8X4),
                 scales=scales[:],
-                in_=grouped[:].rearrange("p b t -> p (b t)"),
+                in_=hid_grouped[n][:].rearrange("p b t -> p (b t)"),
             )
             hid_codes[n], hid_scales[n] = codes, scales
 
@@ -272,18 +279,20 @@ def tile_hiremodule_pa_kernel(tc, x, wh1, gh, bh, wh2, bh2, out):
         w2_grouped = {}
         for step in range(len(regions) + 5):
             run(transpose_x, step)
-            run(quantise_hidden, step - 4)
+            run(regroup_hidden, step - 4)
+            run(first_matmul, step - 1)
             run(copy_x, step)
             run(quantise_x, step)
-            run(first_matmul, step - 1)
-            run(statistics, step - 1)
-            if 1 <= step <= W2_BLOCKS:
-                n = w2_order[step - 1]
-                quantise_weight_block(w2_grouped[n], w2_codes[:, n, :], w2_scales[:, n, :])
-            run(normalise, step - 2)
-            run(transpose_hidden, step - 3)
             if step < W2_BLOCKS:
                 n = w2_order[step]
                 w2_grouped[n] = regroup_weight_block(w2_raw[:, n])
-            run(activate_hidden, step - 3)
+            run(statistics, step - 1)
+            run(transpose_hidden, step - 3)
+            if 1 <= step <= W2_BLOCKS:
+                n = w2_order[step - 1]
+                quantise_weight_block(w2_grouped[n], w2_codes[:, n, :], w2_scales[:, n, :])
+            run(quantise_hidden, step - 4)
             run(second_matmul, step - 5)
+            run(normalise, step - 2)
+            run(activate_hidden, step - 3)
+            run(aggregate, step - 1)

from contextlib import ExitStack

import concourse.mybir as mybir
from concourse.masks import make_identity

F32 = mybir.dt.float32
BF16 = mybir.dt.bfloat16
U32 = mybir.dt.uint32
U8 = mybir.dt.uint8
FP8X4 = mybir.dt.float8_e4m3fn_x4
ACT = mybir.ActivationFunctionType
ALU = mybir.AluOpType

P = 128
PACK = 4
K_PASS = P * PACK
N_TILE = 512

B, H, W, C = 128, 5, 5, 1024
PIXEL = 2
R = 3
K1 = PIXEL * C
F = C // 2
EPS = 1e-6
ROW_PASSES = C // K_PASS
W1_PASSES = K1 // K_PASS
W2_BLOCKS = K1 // N_TILE
ROW_BLOCKS = C // N_TILE

FLOPS = 2 * B * R * W * (K1 * F + F * K1)


def image_row(j, pixel):
    return (j + R * pixel + 3) % H


def tile_hiremodule_pa_kernel(tc, x, wh1, gh, bh, wh2, bh2, out):
    nc = tc.nc
    regions = [(w, j) for w in range(W) for j in range(R)]
    with ExitStack() as ctx:
        ctx.enter_context(tc.manual_schedule())
        consts = ctx.enter_context(tc.tile_pool(name="consts", bufs=1))
        x_pool = ctx.enter_context(tc.tile_pool(name="x_pool", bufs=H * W))
        stage = ctx.enter_context(tc.tile_pool(name="stage", bufs=3))
        work = ctx.enter_context(tc.tile_pool(name="work", bufs=3))
        x_code_pool = ctx.enter_context(tc.tile_pool(name="x_code_pool", bufs=2 * H))
        out_pool = ctx.enter_context(tc.tile_pool(name="out_pool", bufs=6))
        psum_x = ctx.enter_context(tc.psum_pool(name="psum_x", bufs=2))
        psum_u = ctx.enter_context(tc.psum_pool(name="psum_u", bufs=2))
        psum_h = ctx.enter_context(tc.psum_pool(name="psum_h", bufs=1))
        psum_y = ctx.enter_context(tc.psum_pool(name="psum_y", bufs=3))

        def new_rows(j):
            rows = [image_row(j, pixel) for pixel in range(PIXEL)]
            return [h for h in rows if j == 0 or h != image_row(0, 0)]

        x_rows = {}

        def load_x(w):
            for j in range(R):
                for h in new_rows(j):
                    x_row = x_pool.tile([P, C], BF16)
                    nc.sync.dma_start(out=x_row[:], in_=x[:, h, w, :])
                    x_rows[(w, h)] = x_row

        gain_rows = consts.tile([P, P], BF16)
        nc.vector.memset(gain_rows[:], 0.0)
        nc.sync.dma_start(out=gain_rows[0:PACK, :], in_=gh.rearrange("(t p) -> t p", p=P))
        nc.sync.dma_start(out=gain_rows[PACK : 2 * PACK, :], in_=bh.rearrange("(t p) -> t p", p=P))
        w1_raw = consts.tile([P, W1_PASSES, PACK, F], BF16)
        for c in range(W1_PASSES):
            nc.sync.dma_start(
                out=w1_raw[:, c].rearrange("p (u e) f -> p u (e f)", e=2),
                in_=wh1[c * K_PASS : (c + 1) * K_PASS, :].rearrange(
                    "(u p e) f -> p u (e f)", u=2, p=P, e=2
                ),
            )
        load_x(0)
        w2_order = [(k + W2_BLOCKS // 2) % W2_BLOCKS for k in range(W2_BLOCKS)]
        w2_raw = consts.tile([P, W2_BLOCKS, PACK, N_TILE], BF16)

        def load_w2(blocks):
            for n in blocks:
                nc.sync.dma_start(
                    out=w2_raw[:, n],
                    in_=wh2[:, n * N_TILE : (n + 1) * N_TILE].rearrange("(t p) c -> p t c", p=P),
                )

        load_w2(w2_order[: W2_BLOCKS // 2])
        load_x(1)
        load_w2(w2_order[W2_BLOCKS // 2 :])
        bias2 = consts.tile([P, K1], BF16)
        nc.sync.dma_start(out=bias2[:], in_=bh2.partition_broadcast(P))
        for w in range(2, W):
            load_x(w)

        ident = consts.tile([P, P], F32)
        make_identity(nc, ident[:])
        eps = consts.tile([P, 1], F32)
        nc.vector.memset(eps[:], EPS)

        gain_rows_f32 = consts.tile([P, P], F32)
        nc.vector.tensor_copy(out=gain_rows_f32[:], in_=gain_rows[:])
        gain_t = psum_h.tile([P, PACK, P], F32, tag="hid_t")
        nc.tensor.transpose(gain_t[:, 0, :], gain_rows_f32[:], ident[:])
        gain_cols = consts.tile([P, 2 * PACK], F32)
        nc.vector.tensor_copy(out=gain_cols[:], in_=gain_t[:, 0, 0 : 2 * PACK])

        def regroup_weight_block(raw):
            grouped = stage.tile([P, N_TILE, PACK], BF16, align_bytes=64, tag="w_grouped")
            half = N_TILE // 2
            nc.vector.tensor_copy(
                out=grouped[:, :half, :].rearrange("p (c i) t -> p c t i", i=4),
                in_=raw[:, :, :half].rearrange("p t (c i) -> p c t i", i=4),
            )
            nc.scalar.copy(
                out=grouped[:, half:, :].rearrange("p (c i) t -> p c t i", i=4),
                in_=raw[:, :, half:].rearrange("p t (c i) -> p c t i", i=4),
            )
            return grouped

        def quantise_weight_block(grouped, codes, scales):
            nc.vector.quantize_mx(
                out=codes.bitcast(FP8X4),
                scales=scales,
                in_=grouped[:].rearrange("p c t -> p (c t)"),
            )

        w1_codes = consts.tile([P, W1_PASSES, F], U32, align_bytes=64)
        w1_scales = consts.tile([P, W1_PASSES, F], U8, align_bytes=64)
        w1_grouped = {}
        for c in range(W1_PASSES + 1):
            if c < W1_PASSES:
                w1_grouped[c] = regroup_weight_block(w1_raw[:, c])
            if c > 0:
                quantise_weight_block(w1_grouped[c - 1], w1_codes[:, c - 1, :], w1_scales[:, c - 1, :])
        w2_codes = consts.tile([P, W2_BLOCKS, N_TILE], U32, align_bytes=64)
        w2_scales = consts.tile([P, W2_BLOCKS, N_TILE], U8, align_bytes=64)

        x_t, x_grouped, x_codes, x_scales = {}, {}, {}, {}
        u_bank, halves, mean_var, norms = {}, {}, {}, {}
        hid_ts, hid_planes, hid_grouped, hid_codes, hid_scales = {}, {}, {}, {}, {}

        def transpose_x(n):
            w, j = regions[n]
            for h in new_rows(j):
                x_words = x_rows[(w, h)][:].bitcast(F32)
                bank = psum_x.tile([P, 2 * ROW_PASSES, P], F32)
                for q in range(2 * ROW_PASSES):
                    nc.tensor.transpose(bank[:, q, :], x_words[:, q * P : (q + 1) * P], ident[:])
                x_t[(w, h)] = bank

        def copy_x(n):
            w, j = regions[n]
            for h in new_rows(j):
                grouped = stage.tile([P, ROW_PASSES, P, 2], F32, align_bytes=64, tag="x_grouped")
                nc.scalar.copy(
                    out=grouped[:], in_=x_t[(w, h)][:].rearrange("p (g u) b -> p g b u", u=2)
                )
                x_grouped[(w, h)] = grouped

        def quantise_x(n):
            w, j = regions[n]
            for h in new_rows(j):
                codes = x_code_pool.tile([P, ROW_PASSES, P], U32, align_bytes=64, tag="x_codes")
                scales = x_code_pool.tile([P, ROW_PASSES, P], U8, align_bytes=64, tag="x_scales")
                nc.vector.quantize_mx(
                    out=codes[:].rearrange("p g b -> p (g b)").bitcast(FP8X4),
                    scales=scales[:].rearrange("p g b -> p (g b)"),
                    in_=x_grouped[(w, h)][:].rearrange("p g b u -> p (g b u)").bitcast(BF16),
                )
                x_codes[(w, h)], x_scales[(w, h)] = codes, scales

        def first_matmul(n):
            w, j = regions[n]
            u = psum_u.tile([P, F], F32)
            for c in range(W1_PASSES):
                h = image_row(j, c // ROW_PASSES)
                g = c % ROW_PASSES
                nc.tensor.matmul_mx(
                    out=u[:],
                    lhsT=x_codes[(w, h)][:, g, :].bitcast(FP8X4),
                    lhsT_scale=x_scales[(w, h)][:, g, :],
                    rhs=w1_codes[:, c, :].bitcast(FP8X4),
                    rhs_scale=w1_scales[:, c, :],
                    start=(c == 0),
                    stop=(c == W1_PASSES - 1),
                )
            u_bank[n] = u

        def statistics(n):
            stats = work.tile([P, 6], F32)
            nc.vector.bn_stats(out=stats[:], in_=u_bank[n][:])
            halves[n] = stats

        def aggregate(n):
            mv = work.tile([P, 2], F32)
            nc.vector.bn_aggr(out=mv[:], in_=halves[n][:])
            mean_var[n] = mv

        def normalise(n):
            mv = mean_var[n]
            rstd = work.tile([P, 1], F32)
            nc.scalar.activation(
                out=rstd[:], in_=mv[:, 1:2], func=ACT.Abs_reciprocal_sqrt, bias=eps[:]
            )
            shift = work.tile([P, 1], F32)
            nc.scalar.activation(out=shift[:], in_=mv[:, 0:1], func=ACT.Copy, scale=rstd[:])
            nc.scalar.mul(out=shift[:], in_=shift[:], mul=-1.0)
            norm = work.tile([P, F], F32)
            nc.scalar.activation(
                out=norm[:], in_=u_bank[n][:], func=ACT.Identity, scale=rstd[:], bias=shift[:]
            )
            norms[n] = norm

        def transpose_hidden(n):
            hid_t = psum_h.tile([P, PACK, P], F32, tag="hid_t")
            for t in range(PACK):
                nc.tensor.transpose(hid_t[:, t, :], norms[n][:, t * P : (t + 1) * P], ident[:])
            hid_ts[n] = hid_t

        def activate_hidden(n):
            planes = work.tile([P, PACK, P], BF16)
            for t in range(PACK):
                nc.scalar.activation(
                    out=planes[:, t, :], in_=hid_ts[n][:, t, :], func=ACT.Relu,
                    scale=gain_cols[:, t : t + 1], bias=gain_cols[:, PACK + t : PACK + t + 1],
                )
            hid_planes[n] = planes

        def regroup_hidden(n):
            grouped = work.tile([P, P, PACK], BF16, align_bytes=64, tag="hid_grouped")
            nc.vector.tensor_copy(
                out=grouped[:].rearrange("p (c i) t -> p c t i", i=4),
                in_=hid_planes[n][:].rearrange("p t (c i) -> p c t i", i=4),
            )
            hid_grouped[n] = grouped

        def quantise_hidden(n):
            codes = work.tile([P, P], U32, align_bytes=64, tag="hid_codes")
            scales = work.tile([P, P], U8, align_bytes=64, tag="hid_scales")
            nc.vector.quantize_mx(
                out=codes[:].bitcast(FP8X4),
                scales=scales[:],
                in_=hid_grouped[n][:].rearrange("p b t -> p (b t)"),
            )
            hid_codes[n], hid_scales[n] = codes, scales

        def second_matmul(n):
            w, j = regions[n]
            for pixel in range(PIXEL):
                if j == 0 and pixel == 0:
                    continue
                result = out_pool.tile([P, C], F32)
                for half in range(ROW_BLOCKS):
                    block = pixel * ROW_BLOCKS + half
                    y = psum_y.tile([P, N_TILE], F32)
                    nc.tensor.matmul_mx(
                        out=y[:],
                        lhsT=hid_codes[n][:].bitcast(FP8X4),
                        lhsT_scale=hid_scales[n][:],
                        rhs=w2_codes[:, block, :].bitcast(FP8X4),
                        rhs_scale=w2_scales[:, block, :],
                        start=True,
                        stop=True,
                    )
                    nc.vector.tensor_tensor(
                        out=result[:, half * N_TILE : (half + 1) * N_TILE],
                        in0=y[:],
                        in1=bias2[:, block * N_TILE : (block + 1) * N_TILE],
                        op=ALU.add,
                    )
                nc.sync.dma_start(out=out[:, image_row(j, pixel), w, :], in_=result[:])

        def run(stage_of_region, n):
            if 0 <= n < len(regions):
                stage_of_region(n)

        w2_grouped = {}
        for step in range(len(regions) + 5):
            run(transpose_x, step)
            run(regroup_hidden, step - 4)
            run(first_matmul, step - 1)
            run(copy_x, step)
            run(quantise_x, step)
            if step < W2_BLOCKS:
                n = w2_order[step]
                w2_grouped[n] = regroup_weight_block(w2_raw[:, n])
            run(statistics, step - 1)
            run(transpose_hidden, step - 3)
            if 1 <= step <= W2_BLOCKS:
                n = w2_order[step - 1]
                quantise_weight_block(w2_grouped[n], w2_codes[:, n, :], w2_scales[:, n, :])
            run(quantise_hidden, step - 4)
            run(second_matmul, step - 5)
            run(normalise, step - 2)
            run(activate_hidden, step - 3)
            run(aggregate, step - 1)
